import numpy as np
import ml_dtypes


def mxq(x, axis, fmt="e4m3"):
    dtype, down = {"e4m3": (ml_dtypes.float8_e4m3fn, 7), "e5m2": (ml_dtypes.float8_e5m2, 14)}[fmt]
    v = np.moveaxis(np.asarray(x, np.float32).astype(ml_dtypes.bfloat16).astype(np.float64), axis, -1)
    blocks = v.reshape(v.shape[:-1] + (-1, 32))
    amax = np.abs(blocks).max(-1, keepdims=True)
    byte = np.maximum(np.where(amax > 0, np.frexp(amax)[1] - 1 + 127, 0) - down, 1)
    scale = np.exp2(byte - 127.0)
    codes = (blocks / scale).astype(np.float32).astype(dtype).astype(np.float64)
    return np.moveaxis((codes * scale).reshape(v.shape), -1, axis)


WIDE = False


def mx_kscale(k):
    if not WIDE:
        return np.ones(k)
    levels = np.array([10, -10, 5, -5, 0])
    a = np.random.permutation(np.resize(levels, k // 512 * 4)).reshape(k // 512, 4)
    idx = np.arange(k)
    return np.exp2(a[idx // 512, idx % 128 // 32])


BF16 = ml_dtypes.bfloat16


def bf(x):
    return np.asarray(x, np.float32).astype(BF16)


def f64(x):
    return np.asarray(x).astype(np.float64)


E2M1 = np.array([0.0, 0.5, 1.0, 1.5, 2.0, 3.0, 4.0, 6.0, -0.0, -0.5, -1.0, -1.5, -2.0, -3.0, -4.0, -6.0])


def pack_weight(w, fmt):
    k, n = w.shape
    w = f64(bf(w)).reshape(k // 32, 32, n)
    amax = np.abs(w).max(1)
    if fmt == "e4m3":
        byte = np.frexp(amax)[1] - 1 + 127 - 7
    else:
        mant, ex = np.frexp(amax / 6.0)
        byte = np.where(mant > 0.5, ex, ex - 1) + 127
    byte = np.clip(np.where(amax > 0, byte, 1), 1, 254)
    scaled = (w * np.exp2(127.0 - byte)[:, None, :]).reshape(k, n).astype(np.float32)
    by_word = np.ascontiguousarray(scaled.reshape(k // 512, 128, 4, n).transpose(0, 1, 3, 2))
    if fmt == "e4m3":
        words = by_word.astype(ml_dtypes.float8_e4m3fn).view(np.uint8)
    else:
        c = by_word.astype(ml_dtypes.float4_e2m1fn).view(np.uint8) & 0xF
        words = c[..., 0::2] | (c[..., 1::2] << 4)
    return np.ascontiguousarray(words), np.ascontiguousarray(byte.astype(np.uint8).reshape(k // 512, 16, n))


def unpack_weight(words, scales, fmt):
    g, p, n, _ = words.shape
    if fmt == "e4m3":
        vals = np.ascontiguousarray(words).view(ml_dtypes.float8_e4m3fn).astype(np.float64)
    else:
        nib = np.empty((g, p, n, 4), np.uint8)
        nib[..., 0::2] = words & 0xF
        nib[..., 1::2] = words >> 4
        vals = E2M1[nib]
    vals = vals * np.repeat(np.exp2(scales.astype(np.float64) - 127.0), 8, axis=1)[..., None]
    return vals.transpose(0, 1, 3, 2).reshape(g * 512, n)

def pack4(w):
    words, scales = pack_weight(w, "e2m1")
    return words.reshape(words.shape[0], 128, -1), scales


def unpack4(words, scales):
    return unpack_weight(words.reshape(words.shape[0], 128, -1, 2), scales, "e2m1")


B, C, H, W = 1, 512, 64, 32
CH = C // 2
N = H * W
QS = 1.35 * CH ** -0.25


def pool2(t):
    r = t.reshape(B, -1, H // 2, 2, W // 2, 2)
    return r.max(axis=(3, 5)) + r.mean(axis=(3, 5))


def setup_inputs():
    s = mx_kscale(C)
    x = bf(np.random.standard_normal((B, C, H, W)) * s[None, :, None, None])
    w1 = np.random.standard_normal((CH, C)) * QS / np.sqrt(C) / s
    w2 = np.random.standard_normal((CH, C)) * QS / np.sqrt(C) / s
    W1_words, W1_scales = pack4(np.ascontiguousarray(w1.T))
    W2_words, W2_scales = pack4(np.ascontiguousarray(w2.T))
    return {"x": x,
            "W1_words": W1_words, "W1_scales": W1_scales,
            "W2_words": W2_words, "W2_scales": W2_scales}


def reference(x, W1_words, W1_scales, W2_words, W2_scales):
    xq = mxq(f64(x).reshape(B, C, N), 1, "e4m3")
    c1 = unpack4(W1_words, W1_scales).T @ xq
    c2 = unpack4(W2_words, W2_scales).T @ xq
    return pool2(c1.reshape(B, CH, H, W)), c2.reshape(B, CH, H, W)

@@ -1,0 +1,127 @@
+from contextlib import ExitStack
+
+import concourse.mybir as mybir
+
+F32 = mybir.dt.float32
+BF16 = mybir.dt.bfloat16
+I32 = mybir.dt.int32
+U32 = mybir.dt.uint32
+U8 = mybir.dt.uint8
+FP8X4 = mybir.dt.float8_e4m3fn_x4
+FP4X4 = mybir.dt.float4_e2m1fn_x4
+ALU = mybir.AluOpType
+
+P = 128
+PACK = 4
+C_IN = P * PACK
+C_OUT = 256
+HALVES = C_OUT // P
+H, W = 64, 32
+PIXELS = H * W
+CHUNK = 512
+CHUNKS = PIXELS // CHUNK
+ROWS = CHUNK // W
+WINDOWS = CHUNK // 4
+
+FLOPS = 2 * C_IN * 2 * C_OUT * PIXELS
+
+
+def load_scale_rows(nc, plane, scales_dram):
+    for quadrant in range(4):
+        nc.sync.dma_start(
+            out=plane[32 * quadrant : 32 * quadrant + 4, :].bitcast(I32),
+            in_=scales_dram[0, 4 * quadrant : 4 * quadrant + 4, :].bitcast(I32),
+        )
+
+
+def tile_selfspatialattentionmodule_pa_kernel(
+    tc, x, W1_words, W1_scales, W2_words, W2_scales, out_0, out_1
+):
+    nc = tc.nc
+    x_rows = x[0].rearrange("(p t) h w -> p t (h w)", t=PACK)
+    pooled_out = out_0[0].rearrange("(m p) i j -> p m (i j)", p=P)
+    c2_out = out_1[0].rearrange("(m p) h w -> p m (h w)", p=P)
+
+    with ExitStack() as ctx:
+        keep = ctx.enter_context(tc.tile_pool(name="keep", bufs=1))
+        stage = ctx.enter_context(tc.tile_pool(name="stage", bufs=2))
+        psum = ctx.enter_context(tc.psum_pool(name="psum", bufs=4))
+
+        raw = keep.tile([P, CHUNKS, PACK, CHUNK], BF16)
+        w_words = keep.tile([P, 2, 2 * C_OUT], U8, align_bytes=64)
+        w_scales = keep.tile([P, 2, C_OUT], U8, align_bytes=64)
+        x_codes = keep.tile([P, CHUNKS, CHUNK], U32, align_bytes=64)
+        x_scales = keep.tile([P, CHUNKS, CHUNK], U8, align_bytes=64)
+        pooled = keep.tile([P, HALVES, CHUNKS * WINDOWS], F32)
+
+        def load_chunk(c):
+            nc.sync.dma_start(out=raw[:, c], in_=x_rows[:, :, c * CHUNK : (c + 1) * CHUNK])
+
+        nc.vector.memset(w_scales[:].rearrange("p v n -> p (v n)").bitcast(I32), 0)
+        load_chunk(0)
+        nc.sync.dma_start(out=w_words[:, 0, :].bitcast(I32), in_=W1_words[0].bitcast(I32))
+        nc.sync.dma_start(out=w_words[:, 1, :].bitcast(I32), in_=W2_words[0].bitcast(I32))
+        load_scale_rows(nc, w_scales[:, 0, :], W1_scales)
+        load_chunk(1)
+        load_scale_rows(nc, w_scales[:, 1, :], W2_scales)
+        load_chunk(2)
+        load_chunk(3)
+
+        def product(acc, v, m, c):
+            nc.tensor.matmul_mx(
+                out=acc,
+                lhsT=w_words[:, v, 2 * P * m : 2 * P * (m + 1)].bitcast(FP4X4),
+                lhsT_scale=w_scales[:, v, P * m : P * (m + 1)],
+                rhs=x_codes[:, c, :].bitcast(FP8X4),
+                rhs_scale=x_scales[:, c, :],
+                start=True,
+                stop=True,
+            )
+
+        for c in range(CHUNKS):
+            grouped = stage.tile([P, CHUNK, PACK], BF16, align_bytes=64)
+            nc.scalar.copy(
+                out=grouped[:].rearrange("p (n i) t -> p n t i", i=4),
+                in_=raw[:, c].rearrange("p t (n i) -> p n t i", i=4),
+            )
+            nc.vector.quantize_mx(
+                out=x_codes[:, c, :].bitcast(FP8X4),
+                scales=x_scales[:, c, :],
+                in_=grouped[:].rearrange("p n t -> p (n t)"),
+            )
+
+            largest = stage.tile([P, HALVES, WINDOWS], F32)
+            total = stage.tile([P, HALVES, WINDOWS], F32)
+            for m in range(HALVES):
+                c1 = psum.tile([P, CHUNK], F32)
+                product(c1[:], 0, m, c)
+                windows = c1[:].rearrange("p (i a j b) -> p i j a b", i=ROWS // 2, a=2, j=W // 2, b=2)
+                nc.vector.tensor_reduce(
+                    out=largest[:, m, :].rearrange("p (i j) -> p i j", j=W // 2),
+                    in_=windows,
+                    axis=mybir.AxisListType.XY,
+                    op=ALU.max,
+                )
+                nc.vector.tensor_reduce(
+                    out=total[:, m, :].rearrange("p (i j) -> p i j", j=W // 2),
+                    in_=windows,
+                    axis=mybir.AxisListType.XY,
+                    op=ALU.add,
+                )
+            nc.vector.scalar_tensor_tensor(
+                out=pooled[:, :, c * WINDOWS : (c + 1) * WINDOWS],
+                in0=total[:],
+                scalar=0.25,
+                in1=largest[:],
+                op0=ALU.mult,
+                op1=ALU.add,
+            )
+
+            c2_sb = stage.tile([P, HALVES, CHUNK], F32)
+            for m in range(HALVES):
+                c2 = psum.tile([P, CHUNK], F32)
+                product(c2[:], 1, m, c)
+                nc.scalar.copy(out=c2_sb[:, m, :], in_=c2[:])
+            nc.sync.dma_start(out=c2_out[:, :, c * CHUNK : (c + 1) * CHUNK], in_=c2_sb[:])
+
+        nc.sync.dma_start(out=pooled_out, in_=pooled[:])

@@ -20,8 +20,10 @@ H, W = 64, 32
 PIXELS = H * W
 CHUNK = 512
 CHUNKS = PIXELS // CHUNK
-ROWS = CHUNK // W
-WINDOWS = CHUNK // 4
+CORNERS = 4
+WINDOWS = CHUNK // CORNERS
+WIN_ROWS = CHUNK // W // 2
+WIN_COLS = W // 2
 
 FLOPS = 2 * C_IN * 2 * C_OUT * PIXELS
 
@@ -45,7 +47,9 @@ def tile_selfspatialattentionmodule_pa_kernel(
     with ExitStack() as ctx:
         keep = ctx.enter_context(tc.tile_pool(name="keep", bufs=1))
         stage = ctx.enter_context(tc.tile_pool(name="stage", bufs=2))
-        psum = ctx.enter_context(tc.psum_pool(name="psum", bufs=4))
+        store = ctx.enter_context(tc.tile_pool(name="store", bufs=4))
+        psum = ctx.enter_context(tc.psum_pool(name="psum", bufs=3))
+        ctx.enter_context(tc.manual_schedule())
 
         raw = keep.tile([P, CHUNKS, PACK, CHUNK], BF16)
         w_words = keep.tile([P, 2, 2 * C_OUT], U8, align_bytes=64)
@@ -53,9 +57,92 @@ def tile_selfspatialattentionmodule_pa_kernel(
         x_codes = keep.tile([P, CHUNKS, CHUNK], U32, align_bytes=64)
         x_scales = keep.tile([P, CHUNKS, CHUNK], U8, align_bytes=64)
         pooled = keep.tile([P, HALVES, CHUNKS * WINDOWS], F32)
+        grouped = {}
+        c1 = {}
+        c2 = {}
+        totals = {}
+        largest = {}
 
         def load_chunk(c):
             nc.sync.dma_start(out=raw[:, c], in_=x_rows[:, :, c * CHUNK : (c + 1) * CHUNK])
+
+        def regroup(c):
+            grouped[c] = stage.tile([P, CORNERS, WINDOWS, PACK], BF16, align_bytes=64, name="grouped")
+            by_corner = raw[:, c].rearrange(
+                "p t (i a j b) -> p a b i j t", i=WIN_ROWS, a=2, j=WIN_COLS, b=2
+            )
+            for a in range(2):
+                nc.vector.tensor_copy(
+                    out=grouped[c][:, 2 * a].rearrange("p (i j) t -> p i j t", j=WIN_COLS),
+                    in_=by_corner[:, a, 0],
+                )
+                nc.scalar.copy(
+                    out=grouped[c][:, 2 * a + 1].rearrange("p (i j) t -> p i j t", j=WIN_COLS),
+                    in_=by_corner[:, a, 1],
+                )
+
+        def quantise(c):
+            nc.vector.quantize_mx(
+                out=x_codes[:, c, :].bitcast(FP8X4),
+                scales=x_scales[:, c, :],
+                in_=grouped[c][:].rearrange("p q n t -> p (q n t)"),
+            )
+
+        def product(acc, v, m, c, columns, start, stop):
+            nc.tensor.matmul_mx(
+                out=acc,
+                lhsT=w_words[:, v, 2 * P * m : 2 * P * (m + 1)].bitcast(FP4X4),
+                lhsT_scale=w_scales[:, v, P * m : P * (m + 1)],
+                rhs=x_codes[:, c, columns].bitcast(FP8X4),
+                rhs_scale=x_scales[:, c, columns],
+                start=start,
+                stop=stop,
+            )
+
+        def products(c):
+            for m in range(HALVES):
+                c1[c, m] = psum.tile([P, CORNERS, WINDOWS], F32, name="c1")
+                product(c1[c, m][:].rearrange("p q n -> p (q n)"), 0, m, c, slice(0, CHUNK), True, True)
+                c2[c, m] = psum.tile([P, CHUNK], F32, name="c2")
+                product(c2[c, m][:], 1, m, c, slice(0, CHUNK), True, True)
+            totals[c] = psum.tile([P, HALVES, WINDOWS], F32, name="totals", bufs=2)
+            for m in range(HALVES):
+                for q in range(CORNERS):
+                    product(
+                        totals[c][:, m, :], 0, m, c, slice(q * WINDOWS, (q + 1) * WINDOWS),
+                        q == 0, q == CORNERS - 1,
+                    )
+
+        def window_max(c, m):
+            if m == 0:
+                largest[c] = stage.tile([P, HALVES, WINDOWS], F32, name="largest")
+            nc.vector.tensor_reduce(
+                out=largest[c][:, m, :],
+                in_=c1[c, m][:].rearrange("p q n -> p n q"),
+                axis=mybir.AxisListType.X,
+                op=ALU.max,
+            )
+
+        def max_plus_mean(c):
+            nc.vector.scalar_tensor_tensor(
+                out=pooled[:, :, c * WINDOWS : (c + 1) * WINDOWS],
+                in0=totals[c][:],
+                scalar=1.0 / CORNERS,
+                in1=largest[c][:],
+                op0=ALU.mult,
+                op1=ALU.add,
+            )
+            if c % 2 == 1:
+                done = slice((c - 1) * WINDOWS, (c + 1) * WINDOWS)
+                nc.sync.dma_start(out=pooled_out[:, :, done], in_=pooled[:, :, done])
+
+        def store_c2(c, m):
+            c2_sb = store.tile([P, CHUNK], F32)
+            in_image_order = c2_sb[:].rearrange("p (i a j b) -> p a i j b", i=WIN_ROWS, a=2, j=WIN_COLS, b=2)
+            by_corner = c2[c, m][:].rearrange("p (a b i j) -> p a i j b", a=2, b=2, i=WIN_ROWS, j=WIN_COLS)
+            for a in range(2):
+                nc.scalar.copy(out=in_image_order[:, a], in_=by_corner[:, a])
+            nc.sync.dma_start(out=c2_out[:, m, c * CHUNK : (c + 1) * CHUNK], in_=c2_sb[:])
 
         nc.vector.memset(w_scales[:].rearrange("p v n -> p (v n)").bitcast(I32), 0)
         load_chunk(0)
@@ -67,61 +154,18 @@ def tile_selfspatialattentionmodule_pa_kernel(
         load_chunk(2)
         load_chunk(3)
 
-        def product(acc, v, m, c):
-            nc.tensor.matmul_mx(
-                out=acc,
-                lhsT=w_words[:, v, 2 * P * m : 2 * P * (m + 1)].bitcast(FP4X4),
-                lhsT_scale=w_scales[:, v, P * m : P * (m + 1)],
-                rhs=x_codes[:, c, :].bitcast(FP8X4),
-                rhs_scale=x_scales[:, c, :],
-                start=True,
-                stop=True,
-            )
-
+        regroup(0)
+        quantise(0)
+        products(0)
         for c in range(CHUNKS):
-            grouped = stage.tile([P, CHUNK, PACK], BF16, align_bytes=64)
-            nc.scalar.copy(
-                out=grouped[:].rearrange("p (n i) t -> p n t i", i=4),
-                in_=raw[:, c].rearrange("p t (n i) -> p n t i", i=4),
-            )
-            nc.vector.quantize_mx(
-                out=x_codes[:, c, :].bitcast(FP8X4),
-                scales=x_scales[:, c, :],
-                in_=grouped[:].rearrange("p n t -> p (n t)"),
-            )
-
-            largest = stage.tile([P, HALVES, WINDOWS], F32)
-            total = stage.tile([P, HALVES, WINDOWS], F32)
-            for m in range(HALVES):
-                c1 = psum.tile([P, CHUNK], F32)
-                product(c1[:], 0, m, c)
-                windows = c1[:].rearrange("p (i a j b) -> p i j a b", i=ROWS // 2, a=2, j=W // 2, b=2)
-                nc.vector.tensor_reduce(
-                    out=largest[:, m, :].rearrange("p (i j) -> p i j", j=W // 2),
-                    in_=windows,
-                    axis=mybir.AxisListType.XY,
-                    op=ALU.max,
-                )
-                nc.vector.tensor_reduce(
-                    out=total[:, m, :].rearrange("p (i j) -> p i j", j=W // 2),
-                    in_=windows,
-                    axis=mybir.AxisListType.XY,
-                    op=ALU.add,
-                )
-            nc.vector.scalar_tensor_tensor(
-                out=pooled[:, :, c * WINDOWS : (c + 1) * WINDOWS],
-                in0=total[:],
-                scalar=0.25,
-                in1=largest[:],
-                op0=ALU.mult,
-                op1=ALU.add,
-            )
-
-            c2_sb = stage.tile([P, HALVES, CHUNK], F32)
-            for m in range(HALVES):
-                c2 = psum.tile([P, CHUNK], F32)
-                product(c2[:], 1, m, c)
-                nc.scalar.copy(out=c2_sb[:, m, :], in_=c2[:])
-            nc.sync.dma_start(out=c2_out[:, :, c * CHUNK : (c + 1) * CHUNK], in_=c2_sb[:])
-
-        nc.sync.dma_start(out=pooled_out, in_=pooled[:])
+            if c + 1 < CHUNKS:
+                regroup(c + 1)
+            window_max(c, 0)
+            if c + 1 < CHUNKS:
+                quantise(c + 1)
+            window_max(c, 1)
+            max_plus_mean(c)
+            store_c2(c, 0)
+            store_c2(c, 1)
+            if c + 1 < CHUNKS:
+                products(c + 1)

@@ -25,6 +25,8 @@ WINDOWS = CHUNK // CORNERS
 WIN_ROWS = CHUNK // W // 2
 WIN_COLS = W // 2
 
+AHEAD = 2
+
 FLOPS = 2 * C_IN * 2 * C_OUT * PIXELS
 
 
@@ -46,46 +48,42 @@ def tile_selfspatialattentionmodule_pa_kernel(
 
     with ExitStack() as ctx:
         keep = ctx.enter_context(tc.tile_pool(name="keep", bufs=1))
-        stage = ctx.enter_context(tc.tile_pool(name="stage", bufs=2))
-        store = ctx.enter_context(tc.tile_pool(name="store", bufs=4))
         psum = ctx.enter_context(tc.psum_pool(name="psum", bufs=3))
         ctx.enter_context(tc.manual_schedule())
 
         raw = keep.tile([P, CHUNKS, PACK, CHUNK], BF16)
+        grouped = keep.tile([P, CHUNKS, CORNERS, WINDOWS, PACK], BF16, align_bytes=64)
         w_words = keep.tile([P, 2, 2 * C_OUT], U8, align_bytes=64)
         w_scales = keep.tile([P, 2, C_OUT], U8, align_bytes=64)
         x_codes = keep.tile([P, CHUNKS, CHUNK], U32, align_bytes=64)
         x_scales = keep.tile([P, CHUNKS, CHUNK], U8, align_bytes=64)
+        largest = keep.tile([P, CHUNKS, HALVES, WINDOWS], F32)
         pooled = keep.tile([P, HALVES, CHUNKS * WINDOWS], F32)
-        grouped = {}
+        c2_sb = keep.tile([P, CHUNKS, HALVES, CHUNK], F32)
         c1 = {}
         c2 = {}
         totals = {}
-        largest = {}
 
         def load_chunk(c):
             nc.sync.dma_start(out=raw[:, c], in_=x_rows[:, :, c * CHUNK : (c + 1) * CHUNK])
 
         def regroup(c):
-            grouped[c] = stage.tile([P, CORNERS, WINDOWS, PACK], BF16, align_bytes=64, name="grouped")
-            by_corner = raw[:, c].rearrange(
-                "p t (i a j b) -> p a b i j t", i=WIN_ROWS, a=2, j=WIN_COLS, b=2
+            nc.vector.tensor_copy(
+                out=grouped[:, c, 0:2].rearrange("p b (i j) t -> p i j t b", j=WIN_COLS),
+                in_=raw[:, c].rearrange("p t (i a j b) -> p a i j t b", i=WIN_ROWS, a=2, j=WIN_COLS, b=2)[:, 0],
             )
-            for a in range(2):
-                nc.vector.tensor_copy(
-                    out=grouped[c][:, 2 * a].rearrange("p (i j) t -> p i j t", j=WIN_COLS),
-                    in_=by_corner[:, a, 0],
-                )
+            by_corner = raw[:, c].rearrange("p t (i a j b) -> p a b i j t", i=WIN_ROWS, a=2, j=WIN_COLS, b=2)
+            for b in range(2):
                 nc.scalar.copy(
-                    out=grouped[c][:, 2 * a + 1].rearrange("p (i j) t -> p i j t", j=WIN_COLS),
-                    in_=by_corner[:, a, 1],
+                    out=grouped[:, c, 2 + b].rearrange("p (i j) t -> p i j t", j=WIN_COLS),
+                    in_=by_corner[:, 1, b],
                 )
 
         def quantise(c):
             nc.vector.quantize_mx(
                 out=x_codes[:, c, :].bitcast(FP8X4),
                 scales=x_scales[:, c, :],
-                in_=grouped[c][:].rearrange("p q n t -> p (q n t)"),
+                in_=grouped[:, c].rearrange("p q n t -> p (q n t)"),
             )
 
         def product(acc, v, m, c, columns, start, stop):
@@ -103,8 +101,7 @@ def tile_selfspatialattentionmodule_pa_kernel(
             for m in range(HALVES):
                 c1[c, m] = psum.tile([P, CORNERS, WINDOWS], F32, name="c1")
                 product(c1[c, m][:].rearrange("p q n -> p (q n)"), 0, m, c, slice(0, CHUNK), True, True)
-                c2[c, m] = psum.tile([P, CHUNK], F32, name="c2")
-                product(c2[c, m][:], 1, m, c, slice(0, CHUNK), True, True)
+
             totals[c] = psum.tile([P, HALVES, WINDOWS], F32, name="totals", bufs=2)
             for m in range(HALVES):
                 for q in range(CORNERS):
@@ -112,12 +109,13 @@ def tile_selfspatialattentionmodule_pa_kernel(
                         totals[c][:, m, :], 0, m, c, slice(q * WINDOWS, (q + 1) * WINDOWS),
                         q == 0, q == CORNERS - 1,
                     )
+            for m in range(HALVES):
+                c2[c, m] = psum.tile([P, CHUNK], F32, name="c2")
+                product(c2[c, m][:], 1, m, c, slice(0, CHUNK), True, True)
 
         def window_max(c, m):
-            if m == 0:
-                largest[c] = stage.tile([P, HALVES, WINDOWS], F32, name="largest")
             nc.vector.tensor_reduce(
-                out=largest[c][:, m, :],
+                out=largest[:, c, m, :],
                 in_=c1[c, m][:].rearrange("p q n -> p n q"),
                 axis=mybir.AxisListType.X,
                 op=ALU.max,
@@ -128,21 +126,22 @@ def tile_selfspatialattentionmodule_pa_kernel(
                 out=pooled[:, :, c * WINDOWS : (c + 1) * WINDOWS],
                 in0=totals[c][:],
                 scalar=1.0 / CORNERS,
-                in1=largest[c][:],
+                in1=largest[:, c],
                 op0=ALU.mult,
                 op1=ALU.add,
             )
-            if c % 2 == 1:
-                done = slice((c - 1) * WINDOWS, (c + 1) * WINDOWS)
-                nc.sync.dma_start(out=pooled_out[:, :, done], in_=pooled[:, :, done])
 
         def store_c2(c, m):
-            c2_sb = store.tile([P, CHUNK], F32)
-            in_image_order = c2_sb[:].rearrange("p (i a j b) -> p a i j b", i=WIN_ROWS, a=2, j=WIN_COLS, b=2)
+            in_image_order = c2_sb[:, c, m].rearrange("p (i a j b) -> p a i j b", i=WIN_ROWS, a=2, j=WIN_COLS, b=2)
             by_corner = c2[c, m][:].rearrange("p (a b i j) -> p a i j b", a=2, b=2, i=WIN_ROWS, j=WIN_COLS)
             for a in range(2):
                 nc.scalar.copy(out=in_image_order[:, a], in_=by_corner[:, a])
-            nc.sync.dma_start(out=c2_out[:, m, c * CHUNK : (c + 1) * CHUNK], in_=c2_sb[:])
+            nc.sync.dma_start(out=c2_out[:, m, c * CHUNK : (c + 1) * CHUNK], in_=c2_sb[:, c, m])
+
+        def store_pooled(c):
+            if c % 2 == 1:
+                done = slice((c - 1) * WINDOWS, (c + 1) * WINDOWS)
+                nc.sync.dma_start(out=pooled_out[:, :, done], in_=pooled[:, :, done])
 
         nc.vector.memset(w_scales[:].rearrange("p v n -> p (v n)").bitcast(I32), 0)
         load_chunk(0)
@@ -154,18 +153,20 @@ def tile_selfspatialattentionmodule_pa_kernel(
         load_chunk(2)
         load_chunk(3)
 
-        regroup(0)
-        quantise(0)
+        for c in range(AHEAD):
+            regroup(c)
+            quantise(c)
         products(0)
         for c in range(CHUNKS):
-            if c + 1 < CHUNKS:
-                regroup(c + 1)
+            if c + AHEAD < CHUNKS:
+                regroup(c + AHEAD)
             window_max(c, 0)
-            if c + 1 < CHUNKS:
-                quantise(c + 1)
+            if c + AHEAD < CHUNKS:
+                quantise(c + AHEAD)
             window_max(c, 1)
             max_plus_mean(c)
             store_c2(c, 0)
             store_c2(c, 1)
+            store_pooled(c)
             if c + 1 < CHUNKS:
                 products(c + 1)

@@ -25,6 +25,7 @@ WINDOWS = CHUNK // CORNERS
 WIN_ROWS = CHUNK // W // 2
 WIN_COLS = W // 2
 
+VECTOR_ROWS = 6
 AHEAD = 2
 
 FLOPS = 2 * C_IN * 2 * C_OUT * PIXELS
@@ -68,16 +69,12 @@ def tile_selfspatialattentionmodule_pa_kernel(
             nc.sync.dma_start(out=raw[:, c], in_=x_rows[:, :, c * CHUNK : (c + 1) * CHUNK])
 
         def regroup(c):
-            nc.vector.tensor_copy(
-                out=grouped[:, c, 0:2].rearrange("p b (i j) t -> p i j t b", j=WIN_COLS),
-                in_=raw[:, c].rearrange("p t (i a j b) -> p a i j t b", i=WIN_ROWS, a=2, j=WIN_COLS, b=2)[:, 0],
-            )
-            by_corner = raw[:, c].rearrange("p t (i a j b) -> p a b i j t", i=WIN_ROWS, a=2, j=WIN_COLS, b=2)
-            for b in range(2):
-                nc.scalar.copy(
-                    out=grouped[:, c, 2 + b].rearrange("p (i j) t -> p i j t", j=WIN_COLS),
-                    in_=by_corner[:, 1, b],
-                )
+            pairs = raw[:, c].rearrange("p t (i a j b) -> p a i j t b", i=WIN_ROWS, a=2, j=WIN_COLS, b=2)
+            upper = grouped[:, c, 0:2].rearrange("p b (i j) t -> p i j t b", j=WIN_COLS)
+            lower = grouped[:, c, 2:4].rearrange("p b (i j) t -> p i j t b", j=WIN_COLS)
+            nc.vector.tensor_copy(out=upper[:, :VECTOR_ROWS], in_=pairs[:, 0, :VECTOR_ROWS])
+            nc.scalar.copy(out=upper[:, VECTOR_ROWS:], in_=pairs[:, 0, VECTOR_ROWS:])
+            nc.scalar.copy(out=lower, in_=pairs[:, 1])
 
         def quantise(c):
             nc.vector.quantize_mx(
@@ -101,7 +98,8 @@ def tile_selfspatialattentionmodule_pa_kernel(
             for m in range(HALVES):
                 c1[c, m] = psum.tile([P, CORNERS, WINDOWS], F32, name="c1")
                 product(c1[c, m][:].rearrange("p q n -> p (q n)"), 0, m, c, slice(0, CHUNK), True, True)
-
+                c2[c, m] = psum.tile([P, CHUNK], F32, name="c2")
+                product(c2[c, m][:], 1, m, c, slice(0, CHUNK), True, True)
             totals[c] = psum.tile([P, HALVES, WINDOWS], F32, name="totals", bufs=2)
             for m in range(HALVES):
                 for q in range(CORNERS):
@@ -109,9 +107,7 @@ def tile_selfspatialattentionmodule_pa_kernel(
                         totals[c][:, m, :], 0, m, c, slice(q * WINDOWS, (q + 1) * WINDOWS),
                         q == 0, q == CORNERS - 1,
                     )
-            for m in range(HALVES):
-                c2[c, m] = psum.tile([P, CHUNK], F32, name="c2")
-                product(c2[c, m][:], 1, m, c, slice(0, CHUNK), True, True)
+
 
         def window_max(c, m):
             nc.vector.tensor_reduce(
@@ -132,10 +128,10 @@ def tile_selfspatialattentionmodule_pa_kernel(
             )
 
         def store_c2(c, m):
-            in_image_order = c2_sb[:, c, m].rearrange("p (i a j b) -> p a i j b", i=WIN_ROWS, a=2, j=WIN_COLS, b=2)
-            by_corner = c2[c, m][:].rearrange("p (a b i j) -> p a i j b", a=2, b=2, i=WIN_ROWS, j=WIN_COLS)
-            for a in range(2):
-                nc.scalar.copy(out=in_image_order[:, a], in_=by_corner[:, a])
+            nc.scalar.copy(
+                out=c2_sb[:, c, m].rearrange("p (i a j b) -> p i a j b", i=WIN_ROWS, a=2, j=WIN_COLS, b=2),
+                in_=c2[c, m][:].rearrange("p (a b i j) -> p i a j b", a=2, b=2, i=WIN_ROWS, j=WIN_COLS),
+            )
             nc.sync.dma_start(out=c2_out[:, m, c * CHUNK : (c + 1) * CHUNK], in_=c2_sb[:, c, m])
 
         def store_pooled(c):

@@ -142,11 +142,11 @@ def tile_selfspatialattentionmodule_pa_kernel(
         nc.vector.memset(w_scales[:].rearrange("p v n -> p (v n)").bitcast(I32), 0)
         load_chunk(0)
         nc.sync.dma_start(out=w_words[:, 0, :].bitcast(I32), in_=W1_words[0].bitcast(I32))
-        nc.sync.dma_start(out=w_words[:, 1, :].bitcast(I32), in_=W2_words[0].bitcast(I32))
         load_scale_rows(nc, w_scales[:, 0, :], W1_scales)
+        nc.sync.dma_start(out=w_words[:, 1, :].bitcast(I32), in_=W2_words[0].bitcast(I32))
         load_chunk(1)
-        load_scale_rows(nc, w_scales[:, 1, :], W2_scales)
         load_chunk(2)
+        load_scale_rows(nc, w_scales[:, 1, :], W2_scales)
         load_chunk(3)
 
         for c in range(AHEAD):

@@ -25,7 +25,8 @@ WINDOWS = CHUNK // CORNERS
 WIN_ROWS = CHUNK // W // 2
 WIN_COLS = W // 2
 
-VECTOR_ROWS = 6
+VECTOR_ROWS_FILLING = 10
+VECTOR_ROWS = 4
 AHEAD = 2
 
 FLOPS = 2 * C_IN * 2 * C_OUT * PIXELS
@@ -68,13 +69,15 @@ def tile_selfspatialattentionmodule_pa_kernel(
         def load_chunk(c):
             nc.sync.dma_start(out=raw[:, c], in_=x_rows[:, :, c * CHUNK : (c + 1) * CHUNK])
 
-        def regroup(c):
+        def regroup(c, vector_rows):
             pairs = raw[:, c].rearrange("p t (i a j b) -> p a i j t b", i=WIN_ROWS, a=2, j=WIN_COLS, b=2)
-            upper = grouped[:, c, 0:2].rearrange("p b (i j) t -> p i j t b", j=WIN_COLS)
-            lower = grouped[:, c, 2:4].rearrange("p b (i j) t -> p i j t b", j=WIN_COLS)
-            nc.vector.tensor_copy(out=upper[:, :VECTOR_ROWS], in_=pairs[:, 0, :VECTOR_ROWS])
-            nc.scalar.copy(out=upper[:, VECTOR_ROWS:], in_=pairs[:, 0, VECTOR_ROWS:])
-            nc.scalar.copy(out=lower, in_=pairs[:, 1])
+            for a in range(2):
+                corners = grouped[:, c, 2 * a : 2 * a + 2].rearrange("p b (i j) t -> p i j t b", j=WIN_COLS)
+                taken = min(max(vector_rows - a * WIN_ROWS, 0), WIN_ROWS)
+                if taken > 0:
+                    nc.vector.tensor_copy(out=corners[:, :taken], in_=pairs[:, a, :taken])
+                if taken < WIN_ROWS:
+                    nc.scalar.copy(out=corners[:, taken:], in_=pairs[:, a, taken:])
 
         def quantise(c):
             nc.vector.quantize_mx(
@@ -143,23 +146,23 @@ def tile_selfspatialattentionmodule_pa_kernel(
         load_chunk(0)
         nc.sync.dma_start(out=w_words[:, 0, :].bitcast(I32), in_=W1_words[0].bitcast(I32))
         load_scale_rows(nc, w_scales[:, 0, :], W1_scales)
-        nc.sync.dma_start(out=w_words[:, 1, :].bitcast(I32), in_=W2_words[0].bitcast(I32))
         load_chunk(1)
         load_chunk(2)
+        nc.sync.dma_start(out=w_words[:, 1, :].bitcast(I32), in_=W2_words[0].bitcast(I32))
         load_scale_rows(nc, w_scales[:, 1, :], W2_scales)
         load_chunk(3)
 
         for c in range(AHEAD):
-            regroup(c)
+            regroup(c, VECTOR_ROWS_FILLING)
             quantise(c)
         products(0)
         for c in range(CHUNKS):
             if c + AHEAD < CHUNKS:
-                regroup(c + AHEAD)
+                regroup(c + AHEAD, VECTOR_ROWS)
             window_max(c, 0)
+            window_max(c, 1)
             if c + AHEAD < CHUNKS:
                 quantise(c + AHEAD)
-            window_max(c, 1)
             max_plus_mean(c)
             store_c2(c, 0)
             store_c2(c, 1)

@@ -26,8 +26,9 @@ WIN_ROWS = CHUNK // W // 2
 WIN_COLS = W // 2
 
 VECTOR_ROWS_FILLING = 10
-VECTOR_ROWS = 4
 AHEAD = 2
+
+SLOT_START = [0, PACK * CHUNK, PACK * (2 * CHUNK - WINDOWS), PACK * (3 * CHUNK - 2 * WINDOWS)]
 
 FLOPS = 2 * C_IN * 2 * C_OUT * PIXELS
 
@@ -54,7 +55,13 @@ def tile_selfspatialattentionmodule_pa_kernel(
         ctx.enter_context(tc.manual_schedule())
 
         raw = keep.tile([P, CHUNKS, PACK, CHUNK], BF16)
-        grouped = keep.tile([P, CHUNKS, CORNERS, WINDOWS, PACK], BF16, align_bytes=64)
+        grouped_all = keep.tile([P, SLOT_START[CHUNKS - 1] + PACK * CHUNK], BF16, align_bytes=64)
+        grouped = [
+            grouped_all[:, SLOT_START[c] : SLOT_START[c] + PACK * CHUNK].rearrange(
+                "p (q n t) -> p q n t", q=CORNERS, t=PACK
+            )
+            for c in range(CHUNKS)
+        ]
         w_words = keep.tile([P, 2, 2 * C_OUT], U8, align_bytes=64)
         w_scales = keep.tile([P, 2, C_OUT], U8, align_bytes=64)
         x_codes = keep.tile([P, CHUNKS, CHUNK], U32, align_bytes=64)
@@ -72,18 +79,39 @@ def tile_selfspatialattentionmodule_pa_kernel(
         def regroup(c, vector_rows):
             pairs = raw[:, c].rearrange("p t (i a j b) -> p a i j t b", i=WIN_ROWS, a=2, j=WIN_COLS, b=2)
             for a in range(2):
-                corners = grouped[:, c, 2 * a : 2 * a + 2].rearrange("p b (i j) t -> p i j t b", j=WIN_COLS)
+                corners = grouped[c][:, 2 * a : 2 * a + 2].rearrange("p b (i j) t -> p i j t b", j=WIN_COLS)
                 taken = min(max(vector_rows - a * WIN_ROWS, 0), WIN_ROWS)
                 if taken > 0:
                     nc.vector.tensor_copy(out=corners[:, :taken], in_=pairs[:, a, :taken])
                 if taken < WIN_ROWS:
                     nc.scalar.copy(out=corners[:, taken:], in_=pairs[:, a, taken:])
 
+        def regroup_top_right(c):
+            pixels = raw[:, c].rearrange("p t (i a j b) -> p a b i j t", i=WIN_ROWS, a=2, j=WIN_COLS, b=2)
+            nc.vector.tensor_copy(
+                out=grouped[c][:, 1].rearrange("p (i j) t -> p i j t", j=WIN_COLS), in_=pixels[:, 0, 1]
+            )
+
+        def regroup_shared(c):
+            pixels = raw[:, c].rearrange("p t (i a j b) -> p a b i j t", i=WIN_ROWS, a=2, j=WIN_COLS, b=2)
+            nc.gpsimd.tensor_scalar(
+                out=grouped[c][:, 0].rearrange("p (i j) t -> p i j t", j=WIN_COLS),
+                in0=pixels[:, 0, 0],
+                scalar1=1.0,
+                scalar2=0.0,
+                op0=ALU.mult,
+                op1=ALU.add,
+            )
+            pairs = raw[:, c].rearrange("p t (i a j b) -> p a i j t b", i=WIN_ROWS, a=2, j=WIN_COLS, b=2)
+            nc.scalar.copy(
+                out=grouped[c][:, 2:4].rearrange("p b (i j) t -> p i j t b", j=WIN_COLS), in_=pairs[:, 1]
+            )
+
         def quantise(c):
             nc.vector.quantize_mx(
                 out=x_codes[:, c, :].bitcast(FP8X4),
                 scales=x_scales[:, c, :],
-                in_=grouped[:, c].rearrange("p q n t -> p (q n t)"),
+                in_=grouped[c].rearrange("p q n t -> p (q n t)"),
             )
 
         def product(acc, v, m, c, columns, start, stop):
@@ -152,15 +180,19 @@ def tile_selfspatialattentionmodule_pa_kernel(
         load_scale_rows(nc, w_scales[:, 1, :], W2_scales)
         load_chunk(3)
 
-        for c in range(AHEAD):
-            regroup(c, VECTOR_ROWS_FILLING)
-            quantise(c)
+        regroup(0, VECTOR_ROWS_FILLING)
+        quantise(0)
+        regroup(1, VECTOR_ROWS_FILLING)
+        regroup_top_right(2)
+        quantise(1)
         products(0)
         for c in range(CHUNKS):
             if c + AHEAD < CHUNKS:
-                regroup(c + AHEAD, VECTOR_ROWS)
+                regroup_shared(c + AHEAD)
             window_max(c, 0)
             window_max(c, 1)
+            if c + AHEAD + 1 < CHUNKS:
+                regroup_top_right(c + AHEAD + 1)
             if c + AHEAD < CHUNKS:
                 quantise(c + AHEAD)
             max_plus_mean(c)

@@ -69,6 +69,7 @@ def tile_selfspatialattentionmodule_pa_kernel(
         largest = keep.tile([P, CHUNKS, HALVES, WINDOWS], F32)
         pooled = keep.tile([P, HALVES, CHUNKS * WINDOWS], F32)
         c2_sb = keep.tile([P, CHUNKS, HALVES, CHUNK], F32)
+        zeros = keep.tile([P, CHUNK], BF16)
         c1 = {}
         c2 = {}
         totals = {}
@@ -140,6 +141,10 @@ def tile_selfspatialattentionmodule_pa_kernel(
                     )
 
 
+        def warm_up(times, moving):
+            for turn in range(times):
+                nc.tensor.matmul(out=heat[:], lhsT=zeros[:, :P], rhs=moving, start=True, stop=True)
+
         def window_max(c, m):
             nc.vector.tensor_reduce(
                 out=largest[:, c, m, :],
@@ -170,6 +175,8 @@ def tile_selfspatialattentionmodule_pa_kernel(
                 done = slice((c - 1) * WINDOWS, (c + 1) * WINDOWS)
                 nc.sync.dma_start(out=pooled_out[:, :, done], in_=pooled[:, :, done])
 
+        nc.gpsimd.memset(zeros[:], 0.0)
+        heat = psum.tile([P, CHUNK], F32, name="c1")
         nc.vector.memset(w_scales[:].rearrange("p v n -> p (v n)").bitcast(I32), 0)
         load_chunk(0)
         nc.sync.dma_start(out=w_words[:, 0, :].bitcast(I32), in_=W1_words[0].bitcast(I32))
@@ -179,6 +186,10 @@ def tile_selfspatialattentionmodule_pa_kernel(
         nc.sync.dma_start(out=w_words[:, 1, :].bitcast(I32), in_=W2_words[0].bitcast(I32))
         load_scale_rows(nc, w_scales[:, 1, :], W2_scales)
         load_chunk(3)
+
+        warm_up(3, zeros[:])
+        warm_up(2, raw[:, 0, 0, :])
+        warm_up(1, raw[:, 1, 0, :])
 
         regroup(0, VECTOR_ROWS_FILLING)
         quantise(0)

@@ -10,6 +10,7 @@ U8 = mybir.dt.uint8
 FP8X4 = mybir.dt.float8_e4m3fn_x4
 FP4X4 = mybir.dt.float4_e2m1fn_x4
 ALU = mybir.AluOpType
+ACT = mybir.ActivationFunctionType
 
 P = 128
 PACK = 4
@@ -67,6 +68,7 @@ def tile_selfspatialattentionmodule_pa_kernel(
         x_codes = keep.tile([P, CHUNKS, CHUNK], U32, align_bytes=64)
         x_scales = keep.tile([P, CHUNKS, CHUNK], U8, align_bytes=64)
         largest = keep.tile([P, CHUNKS, HALVES, WINDOWS], F32)
+        mean = keep.tile([P, CHUNKS, HALVES, WINDOWS], F32)
         pooled = keep.tile([P, HALVES, CHUNKS * WINDOWS], F32)
         c2_sb = keep.tile([P, CHUNKS, HALVES, CHUNK], F32)
         zeros = keep.tile([P, CHUNK], BF16)
@@ -163,6 +165,12 @@ def tile_selfspatialattentionmodule_pa_kernel(
                 op1=ALU.add,
             )
 
+        def max_plus_mean_elsewhere(c):
+            nc.scalar.activation(out=mean[:, c], in_=totals[c][:], func=ACT.Copy, scale=1.0 / CORNERS)
+            nc.gpsimd.tensor_tensor(
+                out=pooled[:, :, c * WINDOWS : (c + 1) * WINDOWS], in0=largest[:, c], in1=mean[:, c], op=ALU.add
+            )
+
         def store_c2(c, m):
             nc.scalar.copy(
                 out=c2_sb[:, c, m].rearrange("p (i a j b) -> p i a j b", i=WIN_ROWS, a=2, j=WIN_COLS, b=2),
@@ -206,9 +214,12 @@ def tile_selfspatialattentionmodule_pa_kernel(
                 regroup_top_right(c + AHEAD + 1)
             if c + AHEAD < CHUNKS:
                 quantise(c + AHEAD)
-            max_plus_mean(c)
+            if c != 2:
+                max_plus_mean(c)
             store_c2(c, 0)
             store_c2(c, 1)
+            if c == 2:
+                max_plus_mean_elsewhere(c)
             store_pooled(c)
             if c + 1 < CHUNKS:
                 products(c + 1)

@@ -201,7 +201,7 @@ def tile_selfspatialattentionmodule_pa_kernel(
 
         regroup(0, VECTOR_ROWS_FILLING)
         quantise(0)
-        regroup(1, VECTOR_ROWS_FILLING)
+        regroup(1, WIN_ROWS)
         regroup_top_right(2)
         quantise(1)
         products(0)

@@ -110,11 +110,12 @@ def tile_selfspatialattentionmodule_pa_kernel(
                 out=grouped[c][:, 2:4].rearrange("p b (i j) t -> p i j t b", j=WIN_COLS), in_=pairs[:, 1]
             )
 
-        def quantise(c):
+        def quantise(c, first=0, last=CORNERS):
+            columns = slice(first * WINDOWS, last * WINDOWS)
             nc.vector.quantize_mx(
-                out=x_codes[:, c, :].bitcast(FP8X4),
-                scales=x_scales[:, c, :],
-                in_=grouped[c].rearrange("p q n t -> p (q n t)"),
+                out=x_codes[:, c, columns].bitcast(FP8X4),
+                scales=x_scales[:, c, columns],
+                in_=grouped[c][:, first:last].rearrange("p q n t -> p (q n t)"),
             )
 
         def product(acc, v, m, c, columns, start, stop):
@@ -128,12 +129,13 @@ def tile_selfspatialattentionmodule_pa_kernel(
                 stop=stop,
             )
 
-        def products(c):
-            for m in range(HALVES):
-                c1[c, m] = psum.tile([P, CORNERS, WINDOWS], F32, name="c1")
-                product(c1[c, m][:].rearrange("p q n -> p (q n)"), 0, m, c, slice(0, CHUNK), True, True)
-                c2[c, m] = psum.tile([P, CHUNK], F32, name="c2")
-                product(c2[c, m][:], 1, m, c, slice(0, CHUNK), True, True)
+        def convolve(v, m, c, columns=slice(0, CHUNK)):
+            banks = (c1, c2)[v]
+            if (c, m) not in banks:
+                banks[c, m] = psum.tile([P, CHUNK], F32, name=("c1", "c2")[v])
+            product(banks[c, m][:, columns], v, m, c, columns, True, True)
+
+        def window_sums(c):
             totals[c] = psum.tile([P, HALVES, WINDOWS], F32, name="totals", bufs=2)
             for m in range(HALVES):
                 for q in range(CORNERS):
@@ -142,6 +144,19 @@ def tile_selfspatialattentionmodule_pa_kernel(
                         q == 0, q == CORNERS - 1,
                     )
 
+        def first_products():
+            for columns in (slice(0, CHUNK // 2), slice(CHUNK // 2, CHUNK)):
+                for m in range(HALVES):
+                    convolve(0, m, 0, columns)
+            window_sums(0)
+            for m in range(HALVES):
+                convolve(1, m, 0)
+
+        def products(c):
+            for m in range(HALVES):
+                convolve(0, m, c)
+                convolve(1, m, c)
+            window_sums(c)
 
         def warm_up(times, moving):
             for turn in range(times):
@@ -150,7 +165,7 @@ def tile_selfspatialattentionmodule_pa_kernel(
         def window_max(c, m):
             nc.vector.tensor_reduce(
                 out=largest[:, c, m, :],
-                in_=c1[c, m][:].rearrange("p q n -> p n q"),
+                in_=c1[c, m][:].rearrange("p (q n) -> p n q", q=CORNERS),
                 axis=mybir.AxisListType.X,
                 op=ALU.max,
             )
@@ -200,11 +215,12 @@ def tile_selfspatialattentionmodule_pa_kernel(
         warm_up(1, raw[:, 1, 0, :])
 
         regroup(0, VECTOR_ROWS_FILLING)
-        quantise(0)
+        quantise(0, 0, 2)
+        quantise(0, 2, 4)
         regroup(1, WIN_ROWS)
         regroup_top_right(2)
         quantise(1)
-        products(0)
+        first_products()
         for c in range(CHUNKS):
             if c + AHEAD < CHUNKS:
                 regroup_shared(c + AHEAD)

@@ -153,9 +153,10 @@ def tile_selfspatialattentionmodule_pa_kernel(
                 convolve(1, m, 0)
 
         def products(c):
+            order = (1, 0) if c == CHUNKS - 1 else (0, 1)
             for m in range(HALVES):
-                convolve(0, m, c)
-                convolve(1, m, c)
+                for v in order:
+                    convolve(v, m, c)
             window_sums(c)
 
         def warm_up(times, moving):
@@ -170,12 +171,12 @@ def tile_selfspatialattentionmodule_pa_kernel(
                 op=ALU.max,
             )
 
-        def max_plus_mean(c):
+        def max_plus_mean(c, halves):
             nc.vector.scalar_tensor_tensor(
-                out=pooled[:, :, c * WINDOWS : (c + 1) * WINDOWS],
-                in0=totals[c][:],
+                out=pooled[:, halves, c * WINDOWS : (c + 1) * WINDOWS],
+                in0=totals[c][:, halves],
                 scalar=1.0 / CORNERS,
-                in1=largest[:, c],
+                in1=largest[:, c, halves],
                 op0=ALU.mult,
                 op1=ALU.add,
             )
@@ -194,9 +195,8 @@ def tile_selfspatialattentionmodule_pa_kernel(
             nc.sync.dma_start(out=c2_out[:, m, c * CHUNK : (c + 1) * CHUNK], in_=c2_sb[:, c, m])
 
         def store_pooled(c):
-            if c % 2 == 1:
-                done = slice((c - 1) * WINDOWS, (c + 1) * WINDOWS)
-                nc.sync.dma_start(out=pooled_out[:, :, done], in_=pooled[:, :, done])
+            done = slice((c - 1) * WINDOWS, (c + 1) * WINDOWS)
+            nc.sync.dma_start(out=pooled_out[:, :, done], in_=pooled[:, :, done])
 
         nc.gpsimd.memset(zeros[:], 0.0)
         heat = psum.tile([P, CHUNK], F32, name="c1")
@@ -217,7 +217,7 @@ def tile_selfspatialattentionmodule_pa_kernel(
         regroup(0, VECTOR_ROWS_FILLING)
         quantise(0, 0, 2)
         quantise(0, 2, 4)
-        regroup(1, WIN_ROWS)
+        regroup(1, VECTOR_ROWS_FILLING)
         regroup_top_right(2)
         quantise(1)
         first_products()
@@ -230,12 +230,18 @@ def tile_selfspatialattentionmodule_pa_kernel(
                 regroup_top_right(c + AHEAD + 1)
             if c + AHEAD < CHUNKS:
                 quantise(c + AHEAD)
-            if c != 2:
-                max_plus_mean(c)
+            if c == 0:
+                max_plus_mean(c, slice(0, HALVES))
+            elif c == CHUNKS - 1:
+                max_plus_mean(c, slice(0, 1))
+                max_plus_mean(c, slice(1, 2))
             store_c2(c, 0)
-            store_c2(c, 1)
             if c == 2:
+                store_pooled(1)
+            store_c2(c, 1)
+            if c in (1, 2):
                 max_plus_mean_elsewhere(c)
-            store_pooled(c)
+            elif c == 3:
+                store_pooled(3)
             if c + 1 < CHUNKS:
                 products(c + 1)

@@ -27,6 +27,7 @@ WIN_ROWS = CHUNK // W // 2
 WIN_COLS = W // 2
 
 VECTOR_ROWS_FILLING = 10
+RUN = 8
 AHEAD = 2
 
 SLOT_START = [0, PACK * CHUNK, PACK * (2 * CHUNK - WINDOWS), PACK * (3 * CHUNK - 2 * WINDOWS)]
@@ -79,6 +80,15 @@ def tile_selfspatialattentionmodule_pa_kernel(
         def load_chunk(c):
             nc.sync.dma_start(out=raw[:, c], in_=x_rows[:, :, c * CHUNK : (c + 1) * CHUNK])
 
+        def scalar_regroup(c, a, rows):
+            runs = raw[:, c].rearrange("p t (i a k w) -> p a i k t w", i=WIN_ROWS, a=2, w=RUN)
+            slots = grouped[c][:, 2 * a : 2 * a + 2].rearrange(
+                "p b (i k r) t -> p i k t r b", i=WIN_ROWS, r=RUN // 2
+            )
+            nc.scalar.copy(
+                out=slots[:, rows].rearrange("p i k t r b -> p (i k) t r b"), in_=runs[:, a, rows]
+            )
+
         def regroup(c, vector_rows):
             pairs = raw[:, c].rearrange("p t (i a j b) -> p a i j t b", i=WIN_ROWS, a=2, j=WIN_COLS, b=2)
             for a in range(2):
@@ -87,7 +97,7 @@ def tile_selfspatialattentionmodule_pa_kernel(
                 if taken > 0:
                     nc.vector.tensor_copy(out=corners[:, :taken], in_=pairs[:, a, :taken])
                 if taken < WIN_ROWS:
-                    nc.scalar.copy(out=corners[:, taken:], in_=pairs[:, a, taken:])
+                    scalar_regroup(c, a, slice(taken, WIN_ROWS))
 
         def regroup_top_right(c):
             pixels = raw[:, c].rearrange("p t (i a j b) -> p a b i j t", i=WIN_ROWS, a=2, j=WIN_COLS, b=2)
@@ -105,10 +115,7 @@ def tile_selfspatialattentionmodule_pa_kernel(
                 op0=ALU.mult,
                 op1=ALU.add,
             )
-            pairs = raw[:, c].rearrange("p t (i a j b) -> p a i j t b", i=WIN_ROWS, a=2, j=WIN_COLS, b=2)
-            nc.scalar.copy(
-                out=grouped[c][:, 2:4].rearrange("p b (i j) t -> p i j t b", j=WIN_COLS), in_=pairs[:, 1]
-            )
+            scalar_regroup(c, 1, slice(0, WIN_ROWS))
 
         def quantise(c, first=0, last=CORNERS):
             columns = slice(first * WINDOWS, last * WINDOWS)

from contextlib import ExitStack

import concourse.mybir as mybir

F32 = mybir.dt.float32
BF16 = mybir.dt.bfloat16
I32 = mybir.dt.int32
U32 = mybir.dt.uint32
U8 = mybir.dt.uint8
FP8X4 = mybir.dt.float8_e4m3fn_x4
FP4X4 = mybir.dt.float4_e2m1fn_x4
ALU = mybir.AluOpType
ACT = mybir.ActivationFunctionType

P = 128
PACK = 4
C_IN = P * PACK
C_OUT = 256
HALVES = C_OUT // P
H, W = 64, 32
PIXELS = H * W
CHUNK = 512
CHUNKS = PIXELS // CHUNK
CORNERS = 4
WINDOWS = CHUNK // CORNERS
WIN_ROWS = CHUNK // W // 2
WIN_COLS = W // 2

VECTOR_ROWS_FILLING = 10
RUN = 8
AHEAD = 2

SLOT_START = [0, PACK * CHUNK, PACK * (2 * CHUNK - WINDOWS), PACK * (3 * CHUNK - 2 * WINDOWS)]

FLOPS = 2 * C_IN * 2 * C_OUT * PIXELS


def load_scale_rows(nc, plane, scales_dram):
    for quadrant in range(4):
        nc.sync.dma_start(
            out=plane[32 * quadrant : 32 * quadrant + 4, :].bitcast(I32),
            in_=scales_dram[0, 4 * quadrant : 4 * quadrant + 4, :].bitcast(I32),
        )


def tile_selfspatialattentionmodule_pa_kernel(
    tc, x, W1_words, W1_scales, W2_words, W2_scales, out_0, out_1
):
    nc = tc.nc
    x_rows = x[0].rearrange("(p t) h w -> p t (h w)", t=PACK)
    pooled_out = out_0[0].rearrange("(m p) i j -> p m (i j)", p=P)
    c2_out = out_1[0].rearrange("(m p) h w -> p m (h w)", p=P)

    with ExitStack() as ctx:
        keep = ctx.enter_context(tc.tile_pool(name="keep", bufs=1))
        psum = ctx.enter_context(tc.psum_pool(name="psum", bufs=3))
        ctx.enter_context(tc.manual_schedule())

        raw = keep.tile([P, CHUNKS, PACK, CHUNK], BF16)
        grouped_all = keep.tile([P, SLOT_START[CHUNKS - 1] + PACK * CHUNK], BF16, align_bytes=64)
        grouped = [
            grouped_all[:, SLOT_START[c] : SLOT_START[c] + PACK * CHUNK].rearrange(
                "p (q n t) -> p q n t", q=CORNERS, t=PACK
            )
            for c in range(CHUNKS)
        ]
        w_words = keep.tile([P, 2, 2 * C_OUT], U8, align_bytes=64)
        w_scales = keep.tile([P, 2, C_OUT], U8, align_bytes=64)
        x_codes = keep.tile([P, CHUNKS, CHUNK], U32, align_bytes=64)
        x_scales = keep.tile([P, CHUNKS, CHUNK], U8, align_bytes=64)
        largest = keep.tile([P, CHUNKS, HALVES, WINDOWS], F32)
        mean = keep.tile([P, CHUNKS, HALVES, WINDOWS], F32)
        pooled = keep.tile([P, HALVES, CHUNKS * WINDOWS], F32)
        c2_sb = keep.tile([P, CHUNKS, HALVES, CHUNK], F32)
        zeros = keep.tile([P, CHUNK], BF16)
        c1 = {}
        c2 = {}
        totals = {}

        def load_chunk(c):
            nc.sync.dma_start(out=raw[:, c], in_=x_rows[:, :, c * CHUNK : (c + 1) * CHUNK])

        def scalar_regroup(c, a, rows):
            runs = raw[:, c].rearrange("p t (i a k w) -> p a i k t w", i=WIN_ROWS, a=2, w=RUN)
            slots = grouped[c][:, 2 * a : 2 * a + 2].rearrange(
                "p b (i k r) t -> p i k t r b", i=WIN_ROWS, r=RUN // 2
            )
            nc.scalar.copy(
                out=slots[:, rows].rearrange("p i k t r b -> p (i k) t r b"), in_=runs[:, a, rows]
            )

        def regroup(c, vector_rows):
            pairs = raw[:, c].rearrange("p t (i a j b) -> p a i j t b", i=WIN_ROWS, a=2, j=WIN_COLS, b=2)
            for a in range(2):
                corners = grouped[c][:, 2 * a : 2 * a + 2].rearrange("p b (i j) t -> p i j t b", j=WIN_COLS)
                taken = min(max(vector_rows - a * WIN_ROWS, 0), WIN_ROWS)
                if taken > 0:
                    nc.vector.tensor_copy(out=corners[:, :taken], in_=pairs[:, a, :taken])
                if taken < WIN_ROWS:
                    scalar_regroup(c, a, slice(taken, WIN_ROWS))

        def regroup_top_right(c):
            pixels = raw[:, c].rearrange("p t (i a j b) -> p a b i j t", i=WIN_ROWS, a=2, j=WIN_COLS, b=2)
            nc.vector.tensor_copy(
                out=grouped[c][:, 1].rearrange("p (i j) t -> p i j t", j=WIN_COLS), in_=pixels[:, 0, 1]
            )

        def regroup_shared(c):
            pixels = raw[:, c].rearrange("p t (i a j b) -> p a b i j t", i=WIN_ROWS, a=2, j=WIN_COLS, b=2)
            nc.gpsimd.tensor_scalar(
                out=grouped[c][:, 0].rearrange("p (i j) t -> p i j t", j=WIN_COLS),
                in0=pixels[:, 0, 0],
                scalar1=1.0,
                scalar2=0.0,
                op0=ALU.mult,
                op1=ALU.add,
            )
            scalar_regroup(c, 1, slice(0, WIN_ROWS))

        def quantise(c, first=0, last=CORNERS):
            columns = slice(first * WINDOWS, last * WINDOWS)
            nc.vector.quantize_mx(
                out=x_codes[:, c, columns].bitcast(FP8X4),
                scales=x_scales[:, c, columns],
                in_=grouped[c][:, first:last].rearrange("p q n t -> p (q n t)"),
            )

        def product(acc, v, m, c, columns, start, stop):
            nc.tensor.matmul_mx(
                out=acc,
                lhsT=w_words[:, v, 2 * P * m : 2 * P * (m + 1)].bitcast(FP4X4),
                lhsT_scale=w_scales[:, v, P * m : P * (m + 1)],
                rhs=x_codes[:, c, columns].bitcast(FP8X4),
                rhs_scale=x_scales[:, c, columns],
                start=start,
                stop=stop,
            )

        def convolve(v, m, c, columns=slice(0, CHUNK)):
            banks = (c1, c2)[v]
            if (c, m) not in banks:
                banks[c, m] = psum.tile([P, CHUNK], F32, name=("c1", "c2")[v])
            product(banks[c, m][:, columns], v, m, c, columns, True, True)

        def window_sums(c):
            totals[c] = psum.tile([P, HALVES, WINDOWS], F32, name="totals", bufs=2)
            for m in range(HALVES):
                for q in range(CORNERS):
                    product(
                        totals[c][:, m, :], 0, m, c, slice(q * WINDOWS, (q + 1) * WINDOWS),
                        q == 0, q == CORNERS - 1,
                    )

        def first_products():
            for columns in (slice(0, CHUNK // 2), slice(CHUNK // 2, CHUNK)):
                for m in range(HALVES):
                    convolve(0, m, 0, columns)
            window_sums(0)
            for m in range(HALVES):
                convolve(1, m, 0)

        def products(c):
            order = (1, 0) if c == CHUNKS - 1 else (0, 1)
            for m in range(HALVES):
                for v in order:
                    convolve(v, m, c)
            window_sums(c)

        def warm_up(times, moving):
            for turn in range(times):
                nc.tensor.matmul(out=heat[:], lhsT=zeros[:, :P], rhs=moving, start=True, stop=True)

        def window_max(c, m):
            nc.vector.tensor_reduce(
                out=largest[:, c, m, :],
                in_=c1[c, m][:].rearrange("p (q n) -> p n q", q=CORNERS),
                axis=mybir.AxisListType.X,
                op=ALU.max,
            )

        def max_plus_mean(c, halves):
            nc.vector.scalar_tensor_tensor(
                out=pooled[:, halves, c * WINDOWS : (c + 1) * WINDOWS],
                in0=totals[c][:, halves],
                scalar=1.0 / CORNERS,
                in1=largest[:, c, halves],
                op0=ALU.mult,
                op1=ALU.add,
            )

        def max_plus_mean_elsewhere(c):
            nc.scalar.activation(out=mean[:, c], in_=totals[c][:], func=ACT.Copy, scale=1.0 / CORNERS)
            nc.gpsimd.tensor_tensor(
                out=pooled[:, :, c * WINDOWS : (c + 1) * WINDOWS], in0=largest[:, c], in1=mean[:, c], op=ALU.add
            )

        def store_c2(c, m):
            nc.scalar.copy(
                out=c2_sb[:, c, m].rearrange("p (i a j b) -> p i a j b", i=WIN_ROWS, a=2, j=WIN_COLS, b=2),
                in_=c2[c, m][:].rearrange("p (a b i j) -> p i a j b", a=2, b=2, i=WIN_ROWS, j=WIN_COLS),
            )
            nc.sync.dma_start(out=c2_out[:, m, c * CHUNK : (c + 1) * CHUNK], in_=c2_sb[:, c, m])

        def store_pooled(c):
            done = slice((c - 1) * WINDOWS, (c + 1) * WINDOWS)
            nc.sync.dma_start(out=pooled_out[:, :, done], in_=pooled[:, :, done])

        nc.gpsimd.memset(zeros[:], 0.0)
        heat = psum.tile([P, CHUNK], F32, name="c1")
        nc.vector.memset(w_scales[:].rearrange("p v n -> p (v n)").bitcast(I32), 0)
        load_chunk(0)
        nc.sync.dma_start(out=w_words[:, 0, :].bitcast(I32), in_=W1_words[0].bitcast(I32))
        load_scale_rows(nc, w_scales[:, 0, :], W1_scales)
        load_chunk(1)
        load_chunk(2)
        nc.sync.dma_start(out=w_words[:, 1, :].bitcast(I32), in_=W2_words[0].bitcast(I32))
        load_scale_rows(nc, w_scales[:, 1, :], W2_scales)
        load_chunk(3)

        warm_up(3, zeros[:])
        warm_up(2, raw[:, 0, 0, :])
        warm_up(1, raw[:, 1, 0, :])

        regroup(0, VECTOR_ROWS_FILLING)
        quantise(0, 0, 2)
        quantise(0, 2, 4)
        regroup(1, VECTOR_ROWS_FILLING)
        regroup_top_right(2)
        quantise(1)
        first_products()
        for c in range(CHUNKS):
            if c + AHEAD < CHUNKS:
                regroup_shared(c + AHEAD)
            window_max(c, 0)
            window_max(c, 1)
            if c + AHEAD + 1 < CHUNKS:
                regroup_top_right(c + AHEAD + 1)
            if c + AHEAD < CHUNKS:
                quantise(c + AHEAD)
            if c == 0:
                max_plus_mean(c, slice(0, HALVES))
            elif c == CHUNKS - 1:
                max_plus_mean(c, slice(0, 1))
                max_plus_mean(c, slice(1, 2))
            store_c2(c, 0)
            if c == 2:
                store_pooled(1)
            store_c2(c, 1)
            if c in (1, 2):
                max_plus_mean_elsewhere(c)
            elif c == 3:
                store_pooled(3)
            if c + 1 < CHUNKS:
                products(c + 1)
